import numpy as np
import ml_dtypes


def mxq(x, axis, fmt="e4m3"):
    dtype, down = {"e4m3": (ml_dtypes.float8_e4m3fn, 7), "e5m2": (ml_dtypes.float8_e5m2, 14)}[fmt]
    v = np.moveaxis(np.asarray(x, np.float32).astype(ml_dtypes.bfloat16).astype(np.float64), axis, -1)
    blocks = v.reshape(v.shape[:-1] + (-1, 32))
    amax = np.abs(blocks).max(-1, keepdims=True)
    byte = np.maximum(np.where(amax > 0, np.frexp(amax)[1] - 1 + 127, 0) - down, 1)
    scale = np.exp2(byte - 127.0)
    codes = (blocks / scale).astype(np.float32).astype(dtype).astype(np.float64)
    return np.moveaxis((codes * scale).reshape(v.shape), -1, axis)


WIDE = False


def mx_kscale(k):
    if not WIDE:
        return np.ones(k)
    levels = np.array([10, -10, 5, -5, 0])
    a = np.random.permutation(np.resize(levels, k // 512 * 4)).reshape(k // 512, 4)
    idx = np.arange(k)
    return np.exp2(a[idx // 512, idx % 128 // 32])


BF16 = ml_dtypes.bfloat16


def bf(x):
    return np.asarray(x, np.float32).astype(BF16)


def f64(x):
    return np.asarray(x).astype(np.float64)


B, N, DIM, HEADS, DIM_HEAD = 2, 4096, 1024, 2, 64
INNER = HEADS * DIM_HEAD


def setup_inputs():
    s = mx_kscale(DIM)
    return {"x": bf(np.random.standard_normal((B, N, DIM)) * s),
            "W": bf(np.random.standard_normal((3 * INNER, DIM)) / np.sqrt(DIM) / s[None, :])}


def reference(x, W):
    b, n, _ = x.shape
    qkv = mxq(f64(x), 2, "e4m3") @ mxq(f64(W), 1, "e4m3").T
    q, k, v = np.split(qkv, 3, axis=-1)

    def to_heads(t):
        return t.reshape(b, n, HEADS, DIM_HEAD).transpose(0, 2, 1, 3)

    return to_heads(q), to_heads(k), to_heads(v)

@@ -1,0 +1,193 @@
+from contextlib import ExitStack
+
+import concourse.mybir as mybir
+from concourse.masks import make_identity
+
+F32 = mybir.dt.float32
+BF16 = mybir.dt.bfloat16
+U32 = mybir.dt.uint32
+U8 = mybir.dt.uint8
+FP8X4 = mybir.dt.float8_e4m3fn_x4
+
+P = 128
+DIM = 1024
+WORDS = DIM // 2
+TOKENS_PER_BATCH = 4096
+E = 384
+DH = 64
+R = 4
+XBUFS = 9
+CHUNK_T = (16, 16, 16, 8, 4, 4)
+
+FLOPS = 2 * 8192 * DIM * E
+
+
+def tile_get_qkv_t_kernel(tc, x, W, out_0, out_1, out_2):
+    nc = tc.nc
+    outs = (out_0, out_1, out_2)
+    xf = x.flatten_outer_dims()
+
+    chunks = []
+    rounds = []
+    tok = 0
+    for ci, T in enumerate(CHUNK_T):
+        chunks.append((tok // TOKENS_PER_BATCH, tok % TOKENS_PER_BATCH, T, tok))
+        for t0 in range(0, T, R):
+            rounds.append((ci, t0))
+        tok += P * T
+    assert tok == 8192
+    NR = len(rounds)
+
+    with ExitStack() as ctx:
+        const = ctx.enter_context(tc.tile_pool(name="const", bufs=1))
+        xpool = ctx.enter_context(tc.tile_pool(name="xin", bufs=XBUFS))
+        gpool = ctx.enter_context(tc.tile_pool(name="grp", bufs=3))
+        qpool = ctx.enter_context(tc.tile_pool(name="qnt", bufs=3))
+        spool = ctx.enter_context(tc.tile_pool(name="stage", bufs=1))
+        tps = ctx.enter_context(tc.psum_pool(name="tps", bufs=4))
+        ops = ctx.enter_context(tc.psum_pool(name="ops", bufs=4))
+
+        ident = const.tile([P, P], F32, name="ident")
+        make_identity(nc, ident[:])
+
+        ctx.enter_context(tc.manual_schedule())
+
+        xt = {}
+        banks = {}
+        grouped = {}
+        words = {}
+        scales = {}
+        obank = {}
+        stage = {}
+
+        def load(r):
+            ci, t0 = rounds[r]
+            T = chunks[ci][2]
+            tok0 = chunks[ci][3]
+            xt[r] = xpool.tile([P, R * DIM], BF16, name="xt")
+            src = xf[tok0:tok0 + P * T, :].rearrange("(p t) k -> p (t k)", t=T)
+            nc.sync.dma_start(out=xt[r][:], in_=src[:, t0 * DIM:(t0 + R) * DIM])
+
+        def transpose_tile(src_f32, col0):
+            bank = tps.tile([P, 4 * P], F32, name="tb")
+            for q in range(4):
+                nc.tensor.transpose(
+                    bank[:, q * P:(q + 1) * P],
+                    src_f32[:, col0 + q * P:col0 + (q + 1) * P],
+                    ident[:],
+                )
+            return bank
+
+        w_raw = const.tile([P, 3 * DIM], BF16, name="w_raw")
+        nc.sync.dma_start(
+            out=w_raw[:].rearrange("p (a k) -> p a k", a=3),
+            in_=W.rearrange("(a p) k -> p a k", p=P),
+        )
+        for r in range(XBUFS):
+            load(r)
+
+        w_grp = const.tile([P, 2 * E * 2], F32, name="w_grp", align_bytes=64)
+        w_words = const.tile([P, 2 * E], U32, name="w_words", align_bytes=64)
+        w_scales = const.tile([P, 2 * E], U8, name="w_scales", align_bytes=64)
+        w_grp_v = w_grp[:].rearrange("p (g e u) -> p g e u", g=2, u=2)
+        w_f32 = w_raw[:].bitcast(F32)
+        for a in range(3):
+            bank = transpose_tile(w_f32, a * WORDS)
+            nc.scalar.copy(
+                out=w_grp_v[:, :, a * P:(a + 1) * P, :],
+                in_=bank[:].rearrange("p (g u r) -> p g r u", g=2, u=2),
+            )
+        w_bf = w_grp[:].bitcast(BF16)
+        for g in range(2):
+            for c0, c1 in ((0, 256), (256, 384)):
+                nc.vector.quantize_mx(
+                    out=w_words[:, g * E + c0:g * E + c1].bitcast(FP8X4),
+                    scales=w_scales[:, g * E + c0:g * E + c1],
+                    in_=w_bf[:, 4 * (g * E + c0):4 * (g * E + c1)],
+                )
+
+        def transposes(r):
+            xv = xt[r][:].bitcast(F32)
+            banks[r] = [transpose_tile(xv, j * WORDS) for j in range(R)]
+            grouped[r] = gpool.tile([P, R * WORDS], F32, name="grouped", align_bytes=64)
+            words[r] = qpool.tile([P, R * 2 * P], U32, name="words", align_bytes=64)
+            scales[r] = qpool.tile([P, R * 2 * P], U8, name="scales", align_bytes=64)
+
+        def tcopy(r, j):
+            nc.scalar.copy(
+                out=grouped[r][:, j * WORDS:(j + 1) * WORDS].rearrange(
+                    "p (g r u) -> p g r u", g=2, u=2),
+                in_=banks[r][j][:].rearrange("p (g u r) -> p g r u", g=2, u=2),
+            )
+
+        def quant(r, half):
+            n = R * 2 * P // 2
+            nc.vector.quantize_mx(
+                out=words[r][:, half * n:(half + 1) * n].bitcast(FP8X4),
+                scales=scales[r][:, half * n:(half + 1) * n],
+                in_=grouped[r][:].bitcast(BF16)[:, 4 * half * n:4 * (half + 1) * n],
+            )
+
+        def mx(r):
+            obank[r] = []
+            for j in range(R):
+                ob = ops.tile([P, 512], F32, name="ob")
+                obank[r].append(ob)
+                for c0, c1 in ((0, 256), (256, 384)):
+                    for g in range(2):
+                        s0 = j * 2 * P + g * P
+                        nc.tensor.matmul_mx(
+                            out=ob[:, c0:c1],
+                            lhsT=words[r][:, s0:s0 + P].bitcast(FP8X4),
+                            lhsT_scale=scales[r][:, s0:s0 + P],
+                            rhs=w_words[:, g * E + c0:g * E + c1].bitcast(FP8X4),
+                            rhs_scale=w_scales[:, g * E + c0:g * E + c1],
+                            start=(g == 0),
+                            stop=(g == 1),
+                        )
+
+        def ocopy(r, j, on_vector):
+            ci, t0 = rounds[r]
+            T = chunks[ci][2]
+            if ci not in stage:
+                stage[ci] = spool.tile([P, 6 * T * DH], F32, name="stage%d" % ci)
+            dst = stage[ci][:].rearrange("p (s t d) -> p s t d", s=6, d=DH)[:, :, t0 + j, :]
+            src = obank[r][j][:, 0:E].rearrange("p (s d) -> p s d", d=DH)
+            if on_vector:
+                nc.vector.tensor_copy(out=dst, in_=src)
+            else:
+                nc.scalar.copy(out=dst, in_=src)
+
+        def store(ci):
+            b, n0, T, tok0 = chunks[ci]
+            for part in range(3):
+                nc.sync.dma_start(
+                    out=outs[part][b, :, n0:n0 + P * T, :].rearrange(
+                        "h (p t) d -> p h (t d)", t=T),
+                    in_=stage[ci][:, part * 2 * T * DH:(part + 1) * 2 * T * DH].rearrange(
+                        "p (h f) -> p h f", h=2),
+                )
+
+        for it in range(NR + 1):
+            last = it == NR
+            if not last:
+                transposes(it)
+                if it + XBUFS < NR:
+                    load(it + XBUFS)
+                tcopy(it, 0)
+                tcopy(it, 1)
+                quant(it, 0)
+            if it >= 1:
+                mx(it - 1)
+                ocopy(it - 1, 0, True)
+                ocopy(it - 1, 1, not last)
+            if not last:
+                tcopy(it, 2)
+                tcopy(it, 3)
+                quant(it, 1)
+            if it >= 1:
+                ocopy(it - 1, 2, True)
+                ocopy(it - 1, 3, False)
+                ci, t0 = rounds[it - 1]
+                if t0 + R == chunks[ci][2]:
+                    store(ci)

@@ -12,12 +12,14 @@ FP8X4 = mybir.dt.float8_e4m3fn_x4
 P = 128
 DIM = 1024
 WORDS = DIM // 2
-TOKENS_PER_BATCH = 4096
 E = 384
 DH = 64
-R = 4
-XBUFS = 9
-CHUNK_T = (16, 16, 16, 8, 4, 4)
+TPB = 32
+NT = 64
+XT = 8
+XBUFS = 5
+RMAX = 4
+STORES = ((0, 32), (32, 16), (48, 8), (56, 8))
 
 FLOPS = 2 * 8192 * DIM * E
 
@@ -25,23 +27,14 @@ FLOPS = 2 * 8192 * DIM * E
 def tile_get_qkv_t_kernel(tc, x, W, out_0, out_1, out_2):
     nc = tc.nc
     outs = (out_0, out_1, out_2)
-    xf = x.flatten_outer_dims()
-
-    chunks = []
-    rounds = []
-    tok = 0
-    for ci, T in enumerate(CHUNK_T):
-        chunks.append((tok // TOKENS_PER_BATCH, tok % TOKENS_PER_BATCH, T, tok))
-        for t0 in range(0, T, R):
-            rounds.append((ci, t0))
-        tok += P * T
-    assert tok == 8192
-    NR = len(rounds)
+    LOADS = [(0, 1), (1, 1), (2, 2), (4, 4)] + [(i, XT) for i in range(XT, NT, XT)]
+    ROUNDS = [(0, 1), (1, 1), (2, 2)] + [(i, RMAX) for i in range(RMAX, NT, RMAX)]
+    NR = len(ROUNDS)
 
     with ExitStack() as ctx:
         const = ctx.enter_context(tc.tile_pool(name="const", bufs=1))
         xpool = ctx.enter_context(tc.tile_pool(name="xin", bufs=XBUFS))
-        gpool = ctx.enter_context(tc.tile_pool(name="grp", bufs=3))
+        gpool = ctx.enter_context(tc.tile_pool(name="grp", bufs=2))
         qpool = ctx.enter_context(tc.tile_pool(name="qnt", bufs=3))
         spool = ctx.enter_context(tc.tile_pool(name="stage", bufs=1))
         tps = ctx.enter_context(tc.psum_pool(name="tps", bufs=4))
@@ -52,7 +45,7 @@ def tile_get_qkv_t_kernel(tc, x, W, out_0, out_1, out_2):
 
         ctx.enter_context(tc.manual_schedule())
 
-        xt = {}
+        xbuf = {}
         banks = {}
         grouped = {}
         words = {}
@@ -60,13 +53,19 @@ def tile_get_qkv_t_kernel(tc, x, W, out_0, out_1, out_2):
         obank = {}
         stage = {}
 
-        def load(r):
-            ci, t0 = rounds[r]
-            T = chunks[ci][2]
-            tok0 = chunks[ci][3]
-            xt[r] = xpool.tile([P, R * DIM], BF16, name="xt")
-            src = xf[tok0:tok0 + P * T, :].rearrange("(p t) k -> p (t k)", t=T)
-            nc.sync.dma_start(out=xt[r][:], in_=src[:, t0 * DIM:(t0 + R) * DIM])
+        def load(i):
+            g0, n = LOADS[i]
+            b = g0 // TPB
+            t0 = g0 % TPB
+            bi = g0 // XT
+            if bi not in xbuf:
+                xbuf[bi] = xpool.tile([P, XT * DIM], BF16, name="xt")
+            c0 = (g0 % XT) * DIM
+            src = x[b].rearrange("(p t) k -> p (t k)", t=TPB)
+            nc.sync.dma_start(
+                out=xbuf[bi][:, c0:c0 + n * DIM],
+                in_=src[:, t0 * DIM:(t0 + n) * DIM],
+            )
 
         def transpose_tile(src_f32, col0):
             bank = tps.tile([P, 4 * P], F32, name="tb")
@@ -78,13 +77,20 @@ def tile_get_qkv_t_kernel(tc, x, W, out_0, out_1, out_2):
                 )
             return bank
 
+        def copy_out(on_vector, dst, src):
+            if on_vector:
+                nc.vector.tensor_copy(out=dst, in_=src)
+            else:
+                nc.scalar.copy(out=dst, in_=src)
+
         w_raw = const.tile([P, 3 * DIM], BF16, name="w_raw")
-        nc.sync.dma_start(
-            out=w_raw[:].rearrange("p (a k) -> p a k", a=3),
-            in_=W.rearrange("(a p) k -> p a k", p=P),
-        )
-        for r in range(XBUFS):
-            load(r)
+        for a in range(3):
+            nc.sync.dma_start(out=w_raw[:, a * DIM:(a + 1) * DIM], in_=W[a * P:(a + 1) * P, :])
+        n_first = 0
+        for i in range(len(LOADS)):
+            if LOADS[i][0] // XT < XBUFS:
+                load(i)
+                n_first = i + 1
 
         w_grp = const.tile([P, 2 * E * 2], F32, name="w_grp", align_bytes=64)
         w_words = const.tile([P, 2 * E], U32, name="w_words", align_bytes=64)
@@ -93,13 +99,14 @@ def tile_get_qkv_t_kernel(tc, x, W, out_0, out_1, out_2):
         w_f32 = w_raw[:].bitcast(F32)
         for a in range(3):
             bank = transpose_tile(w_f32, a * WORDS)
-            nc.scalar.copy(
-                out=w_grp_v[:, :, a * P:(a + 1) * P, :],
-                in_=bank[:].rearrange("p (g u r) -> p g r u", g=2, u=2),
+            copy_out(
+                a == 1,
+                w_grp_v[:, :, a * P:(a + 1) * P, :],
+                bank[:].rearrange("p (g u r) -> p g r u", g=2, u=2),
             )
         w_bf = w_grp[:].bitcast(BF16)
-        for g in range(2):
-            for c0, c1 in ((0, 256), (256, 384)):
+        for c0, c1 in ((0, 256), (256, 384)):
+            for g in range(2):
                 nc.vector.quantize_mx(
                     out=w_words[:, g * E + c0:g * E + c1].bitcast(FP8X4),
                     scales=w_scales[:, g * E + c0:g * E + c1],
@@ -107,30 +114,31 @@ def tile_get_qkv_t_kernel(tc, x, W, out_0, out_1, out_2):
                 )
 
         def transposes(r):
-            xv = xt[r][:].bitcast(F32)
-            banks[r] = [transpose_tile(xv, j * WORDS) for j in range(R)]
-            grouped[r] = gpool.tile([P, R * WORDS], F32, name="grouped", align_bytes=64)
-            words[r] = qpool.tile([P, R * 2 * P], U32, name="words", align_bytes=64)
-            scales[r] = qpool.tile([P, R * 2 * P], U8, name="scales", align_bytes=64)
+            g0, n = ROUNDS[r]
+            xv = xbuf[g0 // XT][:].bitcast(F32)
+            banks[r] = [transpose_tile(xv, ((g0 + j) % XT) * WORDS) for j in range(n)]
+            grouped[r] = gpool.tile([P, RMAX * WORDS], F32, name="grouped", align_bytes=64)
+            words[r] = qpool.tile([P, RMAX * 2 * P], U32, name="words", align_bytes=64)
+            scales[r] = qpool.tile([P, RMAX * 2 * P], U8, name="scales", align_bytes=64)
 
         def tcopy(r, j):
-            nc.scalar.copy(
-                out=grouped[r][:, j * WORDS:(j + 1) * WORDS].rearrange(
+            copy_out(
+                False,
+                grouped[r][:, j * WORDS:(j + 1) * WORDS].rearrange(
                     "p (g r u) -> p g r u", g=2, u=2),
-                in_=banks[r][j][:].rearrange("p (g u r) -> p g r u", g=2, u=2),
+                banks[r][j][:].rearrange("p (g u r) -> p g r u", g=2, u=2),
             )
 
-        def quant(r, half):
-            n = R * 2 * P // 2
+        def quant(r, j0, j1):
             nc.vector.quantize_mx(
-                out=words[r][:, half * n:(half + 1) * n].bitcast(FP8X4),
-                scales=scales[r][:, half * n:(half + 1) * n],
-                in_=grouped[r][:].bitcast(BF16)[:, 4 * half * n:4 * (half + 1) * n],
+                out=words[r][:, j0 * 2 * P:j1 * 2 * P].bitcast(FP8X4),
+                scales=scales[r][:, j0 * 2 * P:j1 * 2 * P],
+                in_=grouped[r][:].bitcast(BF16)[:, j0 * DIM:j1 * DIM],
             )
 
         def mx(r):
             obank[r] = []
-            for j in range(R):
+            for j in range(ROUNDS[r][1]):
                 ob = ops.tile([P, 512], F32, name="ob")
                 obank[r].append(ob)
                 for c0, c1 in ((0, 256), (256, 384)):
@@ -147,47 +155,54 @@ def tile_get_qkv_t_kernel(tc, x, W, out_0, out_1, out_2):
                         )
 
         def ocopy(r, j, on_vector):
-            ci, t0 = rounds[r]
-            T = chunks[ci][2]
-            if ci not in stage:
-                stage[ci] = spool.tile([P, 6 * T * DH], F32, name="stage%d" % ci)
-            dst = stage[ci][:].rearrange("p (s t d) -> p s t d", s=6, d=DH)[:, :, t0 + j, :]
-            src = obank[r][j][:, 0:E].rearrange("p (s d) -> p s d", d=DH)
-            if on_vector:
-                nc.vector.tensor_copy(out=dst, in_=src)
-            else:
-                nc.scalar.copy(out=dst, in_=src)
+            gt = ROUNDS[r][0] + j
+            b = gt // TPB
+            if b not in stage:
+                stage[b] = spool.tile([P, 6 * TPB * DH], F32, name="stage%d" % b)
+            copy_out(
+                on_vector,
+                stage[b][:].rearrange("p (s t d) -> p s t d", s=6, d=DH)[:, :, gt % TPB, :],
+                obank[r][j][:, 0:E].rearrange("p (s d) -> p s d", d=DH),
+            )
 
-        def store(ci):
-            b, n0, T, tok0 = chunks[ci]
+        def store(g0, n):
+            b = g0 // TPB
+            t0 = g0 % TPB
+            sv = stage[b][:].rearrange("p (s t d) -> p s t d", s=6, d=DH)
             for part in range(3):
                 nc.sync.dma_start(
-                    out=outs[part][b, :, n0:n0 + P * T, :].rearrange(
-                        "h (p t) d -> p h (t d)", t=T),
-                    in_=stage[ci][:, part * 2 * T * DH:(part + 1) * 2 * T * DH].rearrange(
-                        "p (h f) -> p h f", h=2),
+                    out=outs[part][b].rearrange("h (p t) d -> p h t d", t=TPB)[:, :, t0:t0 + n, :],
+                    in_=sv[:, 2 * part:2 * part + 2, t0:t0 + n, :],
                 )
 
+        next_load = n_first
         for it in range(NR + 1):
             last = it == NR
             if not last:
+                g0, n = ROUNDS[it]
+                h = (n + 1) // 2
                 transposes(it)
-                if it + XBUFS < NR:
-                    load(it + XBUFS)
-                tcopy(it, 0)
-                tcopy(it, 1)
-                quant(it, 0)
+                if (g0 + n) % XT == 0 and next_load < len(LOADS):
+                    load(next_load)
+                    next_load += 1
+                for j in range(h):
+                    tcopy(it, j)
+                quant(it, 0, h)
             if it >= 1:
+                pn = ROUNDS[it - 1][1]
+                ph = (pn + 1) // 2
                 mx(it - 1)
-                ocopy(it - 1, 0, True)
-                ocopy(it - 1, 1, not last)
+                for j in range(ph):
+                    ocopy(it - 1, j, (j == 0) or not last)
             if not last:
-                tcopy(it, 2)
-                tcopy(it, 3)
-                quant(it, 1)
+                for j in range(h, n):
+                    tcopy(it, j)
+                if n > h:
+                    quant(it, h, n)
             if it >= 1:
-                ocopy(it - 1, 2, True)
-                ocopy(it - 1, 3, False)
-                ci, t0 = rounds[it - 1]
-                if t0 + R == chunks[ci][2]:
-                    store(ci)
+                for j in range(ph, pn):
+                    ocopy(it - 1, j, j < pn - 1)
+                done = ROUNDS[it - 1][0] + pn
+                for g0s, ns in STORES:
+                    if g0s + ns == done:
+                        store(g0s, ns)

@@ -27,8 +27,8 @@ FLOPS = 2 * 8192 * DIM * E
 def tile_get_qkv_t_kernel(tc, x, W, out_0, out_1, out_2):
     nc = tc.nc
     outs = (out_0, out_1, out_2)
-    LOADS = [(0, 1), (1, 1), (2, 2), (4, 4)] + [(i, XT) for i in range(XT, NT, XT)]
-    ROUNDS = [(0, 1), (1, 1), (2, 2)] + [(i, RMAX) for i in range(RMAX, NT, RMAX)]
+    LOADS = [(0, 2), (2, 2), (4, 4), (8, 4), (12, 4)] + [(i, XT) for i in range(2 * XT, NT, XT)]
+    ROUNDS = [(0, 2), (2, 2)] + [(i, RMAX) for i in range(RMAX, NT, RMAX)]
     NR = len(ROUNDS)
 
     with ExitStack() as ctx:

@@ -19,7 +19,7 @@ NT = 64
 XT = 8
 XBUFS = 5
 RMAX = 4
-STORES = ((0, 32), (32, 16), (48, 8), (56, 8))
+STORES = ((0, 32), (32, 16), (48, 8), (56, 4), (60, 4))
 
 FLOPS = 2 * 8192 * DIM * E
 

from contextlib import ExitStack

import concourse.mybir as mybir
from concourse.masks import make_identity

F32 = mybir.dt.float32
BF16 = mybir.dt.bfloat16
U32 = mybir.dt.uint32
U8 = mybir.dt.uint8
FP8X4 = mybir.dt.float8_e4m3fn_x4

P = 128
DIM = 1024
WORDS = DIM // 2
E = 384
DH = 64
TPB = 32
NT = 64
XT = 8
XBUFS = 5
RMAX = 4
STORES = ((0, 32), (32, 16), (48, 8), (56, 4), (60, 4))

FLOPS = 2 * 8192 * DIM * E


def tile_get_qkv_t_kernel(tc, x, W, out_0, out_1, out_2):
    nc = tc.nc
    outs = (out_0, out_1, out_2)
    LOADS = [(0, 2), (2, 2), (4, 4), (8, 4), (12, 4)] + [(i, XT) for i in range(2 * XT, NT, XT)]
    ROUNDS = [(0, 2), (2, 2)] + [(i, RMAX) for i in range(RMAX, NT, RMAX)]
    NR = len(ROUNDS)

    with ExitStack() as ctx:
        const = ctx.enter_context(tc.tile_pool(name="const", bufs=1))
        xpool = ctx.enter_context(tc.tile_pool(name="xin", bufs=XBUFS))
        gpool = ctx.enter_context(tc.tile_pool(name="grp", bufs=2))
        qpool = ctx.enter_context(tc.tile_pool(name="qnt", bufs=3))
        spool = ctx.enter_context(tc.tile_pool(name="stage", bufs=1))
        tps = ctx.enter_context(tc.psum_pool(name="tps", bufs=4))
        ops = ctx.enter_context(tc.psum_pool(name="ops", bufs=4))

        ident = const.tile([P, P], F32, name="ident")
        make_identity(nc, ident[:])

        ctx.enter_context(tc.manual_schedule())

        xbuf = {}
        banks = {}
        grouped = {}
        words = {}
        scales = {}
        obank = {}
        stage = {}

        def load(i):
            g0, n = LOADS[i]
            b = g0 // TPB
            t0 = g0 % TPB
            bi = g0 // XT
            if bi not in xbuf:
                xbuf[bi] = xpool.tile([P, XT * DIM], BF16, name="xt")
            c0 = (g0 % XT) * DIM
            src = x[b].rearrange("(p t) k -> p (t k)", t=TPB)
            nc.sync.dma_start(
                out=xbuf[bi][:, c0:c0 + n * DIM],
                in_=src[:, t0 * DIM:(t0 + n) * DIM],
            )

        def transpose_tile(src_f32, col0):
            bank = tps.tile([P, 4 * P], F32, name="tb")
            for q in range(4):
                nc.tensor.transpose(
                    bank[:, q * P:(q + 1) * P],
                    src_f32[:, col0 + q * P:col0 + (q + 1) * P],
                    ident[:],
                )
            return bank

        def copy_out(on_vector, dst, src):
            if on_vector:
                nc.vector.tensor_copy(out=dst, in_=src)
            else:
                nc.scalar.copy(out=dst, in_=src)

        w_raw = const.tile([P, 3 * DIM], BF16, name="w_raw")
        for a in range(3):
            nc.sync.dma_start(out=w_raw[:, a * DIM:(a + 1) * DIM], in_=W[a * P:(a + 1) * P, :])
        n_first = 0
        for i in range(len(LOADS)):
            if LOADS[i][0] // XT < XBUFS:
                load(i)
                n_first = i + 1

        w_grp = const.tile([P, 2 * E * 2], F32, name="w_grp", align_bytes=64)
        w_words = const.tile([P, 2 * E], U32, name="w_words", align_bytes=64)
        w_scales = const.tile([P, 2 * E], U8, name="w_scales", align_bytes=64)
        w_grp_v = w_grp[:].rearrange("p (g e u) -> p g e u", g=2, u=2)
        w_f32 = w_raw[:].bitcast(F32)
        for a in range(3):
            bank = transpose_tile(w_f32, a * WORDS)
            copy_out(
                a == 1,
                w_grp_v[:, :, a * P:(a + 1) * P, :],
                bank[:].rearrange("p (g u r) -> p g r u", g=2, u=2),
            )
        w_bf = w_grp[:].bitcast(BF16)
        for c0, c1 in ((0, 256), (256, 384)):
            for g in range(2):
                nc.vector.quantize_mx(
                    out=w_words[:, g * E + c0:g * E + c1].bitcast(FP8X4),
                    scales=w_scales[:, g * E + c0:g * E + c1],
                    in_=w_bf[:, 4 * (g * E + c0):4 * (g * E + c1)],
                )

        def transposes(r):
            g0, n = ROUNDS[r]
            xv = xbuf[g0 // XT][:].bitcast(F32)
            banks[r] = [transpose_tile(xv, ((g0 + j) % XT) * WORDS) for j in range(n)]
            grouped[r] = gpool.tile([P, RMAX * WORDS], F32, name="grouped", align_bytes=64)
            words[r] = qpool.tile([P, RMAX * 2 * P], U32, name="words", align_bytes=64)
            scales[r] = qpool.tile([P, RMAX * 2 * P], U8, name="scales", align_bytes=64)

        def tcopy(r, j):
            copy_out(
                False,
                grouped[r][:, j * WORDS:(j + 1) * WORDS].rearrange(
                    "p (g r u) -> p g r u", g=2, u=2),
                banks[r][j][:].rearrange("p (g u r) -> p g r u", g=2, u=2),
            )

        def quant(r, j0, j1):
            nc.vector.quantize_mx(
                out=words[r][:, j0 * 2 * P:j1 * 2 * P].bitcast(FP8X4),
                scales=scales[r][:, j0 * 2 * P:j1 * 2 * P],
                in_=grouped[r][:].bitcast(BF16)[:, j0 * DIM:j1 * DIM],
            )

        def mx(r):
            obank[r] = []
            for j in range(ROUNDS[r][1]):
                ob = ops.tile([P, 512], F32, name="ob")
                obank[r].append(ob)
                for c0, c1 in ((0, 256), (256, 384)):
                    for g in range(2):
                        s0 = j * 2 * P + g * P
                        nc.tensor.matmul_mx(
                            out=ob[:, c0:c1],
                            lhsT=words[r][:, s0:s0 + P].bitcast(FP8X4),
                            lhsT_scale=scales[r][:, s0:s0 + P],
                            rhs=w_words[:, g * E + c0:g * E + c1].bitcast(FP8X4),
                            rhs_scale=w_scales[:, g * E + c0:g * E + c1],
                            start=(g == 0),
                            stop=(g == 1),
                        )

        def ocopy(r, j, on_vector):
            gt = ROUNDS[r][0] + j
            b = gt // TPB
            if b not in stage:
                stage[b] = spool.tile([P, 6 * TPB * DH], F32, name="stage%d" % b)
            copy_out(
                on_vector,
                stage[b][:].rearrange("p (s t d) -> p s t d", s=6, d=DH)[:, :, gt % TPB, :],
                obank[r][j][:, 0:E].rearrange("p (s d) -> p s d", d=DH),
            )

        def store(g0, n):
            b = g0 // TPB
            t0 = g0 % TPB
            sv = stage[b][:].rearrange("p (s t d) -> p s t d", s=6, d=DH)
            for part in range(3):
                nc.sync.dma_start(
                    out=outs[part][b].rearrange("h (p t) d -> p h t d", t=TPB)[:, :, t0:t0 + n, :],
                    in_=sv[:, 2 * part:2 * part + 2, t0:t0 + n, :],
                )

        next_load = n_first
        for it in range(NR + 1):
            last = it == NR
            if not last:
                g0, n = ROUNDS[it]
                h = (n + 1) // 2
                transposes(it)
                if (g0 + n) % XT == 0 and next_load < len(LOADS):
                    load(next_load)
                    next_load += 1
                for j in range(h):
                    tcopy(it, j)
                quant(it, 0, h)
            if it >= 1:
                pn = ROUNDS[it - 1][1]
                ph = (pn + 1) // 2
                mx(it - 1)
                for j in range(ph):
                    ocopy(it - 1, j, (j == 0) or not last)
            if not last:
                for j in range(h, n):
                    tcopy(it, j)
                if n > h:
                    quant(it, h, n)
            if it >= 1:
                for j in range(ph, pn):
                    ocopy(it - 1, j, j < pn - 1)
                done = ROUNDS[it - 1][0] + pn
                for g0s, ns in STORES:
                    if g0s + ns == done:
                        store(g0s, ns)
